import numpy as np
import ml_dtypes


def mxq(x, axis, fmt="e4m3"):
    dtype, down = {"e4m3": (ml_dtypes.float8_e4m3fn, 7), "e5m2": (ml_dtypes.float8_e5m2, 14)}[fmt]
    v = np.moveaxis(np.asarray(x, np.float32).astype(ml_dtypes.bfloat16).astype(np.float64), axis, -1)
    blocks = v.reshape(v.shape[:-1] + (-1, 32))
    amax = np.abs(blocks).max(-1, keepdims=True)
    byte = np.maximum(np.where(amax > 0, np.frexp(amax)[1] - 1 + 127, 0) - down, 1)
    scale = np.exp2(byte - 127.0)
    codes = (blocks / scale).astype(np.float32).astype(dtype).astype(np.float64)
    return np.moveaxis((codes * scale).reshape(v.shape), -1, axis)


WIDE = False


def mx_kscale(k):
    if not WIDE:
        return np.ones(k)
    levels = np.array([10, -10, 5, -5, 0])
    a = np.random.permutation(np.resize(levels, k // 512 * 4)).reshape(k // 512, 4)
    idx = np.arange(k)
    return np.exp2(a[idx // 512, idx % 128 // 32])


BF16 = ml_dtypes.bfloat16


def bf(x):
    return np.asarray(x, np.float32).astype(BF16)


def f64(x):
    return np.asarray(x).astype(np.float64)


B, S, H, D, KV = 1, 640, 32, 128, 512


def setup_inputs():
    g = np.concatenate([np.full(D, 1.25), np.full(D, 1.25), np.full(D, 2.0)])
    x = np.random.standard_normal((B, S, H, 3 * D)) * g
    s = np.ones(S)
    s[:KV] = mx_kscale(KV)
    x[..., 0] = 8.0
    x[..., D] += (np.log(s) * np.sqrt(D) / 8.0)[None, :, None]
    x[..., 2 * D:] *= (s.max() / s)[None, :, None, None]
    return {"qkv": bf(x), "kv_seq_len": KV}


def reference(qkv, kv_seq_len):
    q, k, v = np.split(f64(qkv), 3, axis=-1)
    q, k, v = (a.transpose(0, 2, 1, 3) for a in (q, k, v))
    kv_mask = np.arange(S) < kv_seq_len
    k, v = k[:, :, kv_mask], v[:, :, kv_mask]
    scores = q @ k.transpose(0, 1, 3, 2) * (1.0 / np.sqrt(D))
    e = np.exp(scores - scores.max(-1, keepdims=True))
    out = (mxq(e, 3, "e4m3") @ mxq(v, 2, "e4m3")) / e.sum(-1, keepdims=True)
    return out.transpose(0, 2, 1, 3)

@@ -1,0 +1,252 @@
+import math
+
+import concourse.mybir as mybir
+from concourse.masks import make_identity
+
+F32 = mybir.dt.float32
+BF16 = mybir.dt.bfloat16
+U32 = mybir.dt.uint32
+U8 = mybir.dt.uint8
+FP8X4 = mybir.dt.float8_e4m3fn_x4
+EXP = mybir.ActivationFunctionType.Exp
+MAX = mybir.AluOpType.max
+MULT = mybir.AluOpType.mult
+X = mybir.AxisListType.X
+
+P = 128
+PACK = 4
+POSITIONS = 640
+HEADS = 32
+D = 128
+KEYS = 512
+Q_BLOCKS = POSITIONS // P
+K_BLOCKS = KEYS // P
+GROUP = 4
+GROUPS = HEADS // GROUP
+ROUNDS = GROUPS * Q_BLOCKS
+PAIRS = ((0, 1), (2, 3))
+SCALE = 1.0 / math.sqrt(D)
+
+FLOPS = 2 * 2 * HEADS * POSITIONS * KEYS * D
+BYTES = 2 * HEADS * D * (POSITIONS + 2 * KEYS) + 4 * HEADS * D * POSITIONS
+
+
+def tile_attention_kernel(tc, qkv, kv_seq_len, out):
+    nc = tc.nc
+    assert kv_seq_len == KEYS
+
+    with tc.tile_pool(name="const", bufs=1) as const, tc.tile_pool(name="raw", bufs=3) as raw, tc.tile_pool(
+        name="group", bufs=2
+    ) as group, tc.tile_pool(name="work", bufs=2) as work, tc.psum_pool(name="psum", bufs=1) as psum:
+        ident_bf16 = const.tile([P, P], BF16)
+        make_identity(nc, ident_bf16[:])
+        ident_f32 = const.tile([P, P], F32)
+        make_identity(nc, ident_f32[:])
+
+        qk_raw = {}
+        v_raw = {}
+        q_t = {}
+        k_t = {}
+        v_codes = {}
+        v_scales = {}
+        prep_bank = {}
+        v_grouped = {}
+        scores = {}
+        e_rows = {}
+        neg_max = {}
+        row_sum = {}
+        e_t_bank = {}
+        e_grouped = {}
+        e_codes = {}
+        e_scales = {}
+        out_bank = {}
+
+        def load_group(g):
+            if g >= GROUPS:
+                return
+            heads = slice(GROUP * g, GROUP * g + GROUP)
+            qk_raw[g] = raw.tile([P, Q_BLOCKS, GROUP, 2 * D], BF16, name="qk_raw")
+            v_raw[g] = raw.tile([P, PACK, GROUP, D], BF16, name="v_raw")
+            for b in range(K_BLOCKS):
+                nc.sync.dma_start(out=qk_raw[g][:, b], in_=qkv[0, P * b : P * b + P, heads, 0 : 2 * D])
+            for t in range(PACK):
+                first = 256 * (t // 2) + t % 2
+                nc.sync.dma_start(out=v_raw[g][:, t], in_=qkv[0, first : first + 256 : 2, heads, 2 * D : 3 * D])
+            b = K_BLOCKS
+            nc.sync.dma_start(out=qk_raw[g][:, b, :, 0:D], in_=qkv[0, P * b : P * b + P, heads, 0:D])
+
+        def open_group(g):
+            q_t[g] = group.tile([P, Q_BLOCKS, GROUP, P], BF16, name="q_t")
+            k_t[g] = group.tile([P, GROUP, K_BLOCKS, P], BF16, name="k_t")
+            v_codes[g] = group.tile([P, GROUP, D], U32, name="v_codes", align_bytes=64)
+            v_scales[g] = group.tile([P, GROUP, D], U8, name="v_scales", align_bytes=64)
+
+        def transpose_qk(g, b):
+            if g >= GROUPS:
+                return
+            if b == 0:
+                open_group(g)
+            prep_bank[g, b] = psum.tile([P, 2, GROUP, P], BF16, name="prep_bank")
+            for part in range(2 if b < K_BLOCKS else 1):
+                for h in range(GROUP):
+                    nc.tensor.transpose(
+                        prep_bank[g, b][:, part, h, :], qk_raw[g][:, b, h, D * part : D * part + D], ident_bf16[:]
+                    )
+
+        def keep_q(g, b):
+            if g < GROUPS:
+                nc.scalar.copy(out=q_t[g][:, b], in_=prep_bank[g, b][:, 0])
+
+        def keep_k(g, b):
+            if g < GROUPS and b < K_BLOCKS:
+                nc.scalar.copy(out=k_t[g][:, :, b, :], in_=prep_bank[g, b][:, 1])
+
+        def group_v(g, h):
+            if g < GROUPS and h < GROUP:
+                v_grouped[g, h] = work.tile([P, D, PACK], BF16, name="v_grouped", align_bytes=64)
+                nc.vector.tensor_copy(out=v_grouped[g, h][:], in_=v_raw[g][:, :, h, :].rearrange("p t d -> p d t"))
+
+        def quantise_v(g, h):
+            if g < GROUPS and h < GROUP:
+                nc.vector.quantize_mx(
+                    out=v_codes[g][:, h, :].bitcast(FP8X4),
+                    scales=v_scales[g][:, h, :],
+                    in_=v_grouped[g, h][:].rearrange("p d t -> p (d t)"),
+                )
+
+        def live(r):
+            return 0 <= r < ROUNDS
+
+        def score(r, h):
+            if not live(r):
+                return
+            g, i = divmod(r, Q_BLOCKS)
+            scores[r, h] = psum.tile([P, KEYS], F32, name="scores", bufs=4)
+            nc.tensor.matmul(
+                out=scores[r, h][:],
+                lhsT=q_t[g][:, i, h, :],
+                rhs=k_t[g][:, h].rearrange("d b k -> d (b k)"),
+                start=True,
+                stop=True,
+            )
+
+        def row_max(r, pair):
+            if not live(r):
+                return
+            top = work.tile([P, 2], F32, name="top", bufs=4)
+            for j, h in enumerate(pair):
+                nc.vector.tensor_reduce(out=top[:, j : j + 1], in_=scores[r, h][:], axis=X, op=MAX)
+            neg_max[r, pair] = work.tile([P, 2], F32, name="neg_max", bufs=4)
+            nc.vector.tensor_scalar_mul(out=neg_max[r, pair][:], in0=top[:], scalar1=-SCALE)
+
+        def exponent(r, pair):
+            if not live(r):
+                return
+            if pair == PAIRS[0]:
+                row_sum[r] = work.tile([P, GROUP], F32, name="row_sum", bufs=4)
+            for j, h in enumerate(pair):
+                e_rows[r, h] = work.tile([P, KEYS], BF16, name="e_rows", bufs=6)
+                nc.scalar.activation(
+                    out=e_rows[r, h][:],
+                    in_=scores[r, h][:],
+                    func=EXP,
+                    bias=neg_max[r, pair][:, j : j + 1],
+                    scale=SCALE,
+                    accum_out=row_sum[r][:, h : h + 1],
+                )
+
+        def transpose_e(r, pair):
+            if not live(r):
+                return
+            e_t_bank[r, pair] = psum.tile([P, 2, 2, P], F32, name="e_t_bank", bufs=2)
+            for j, h in enumerate(pair):
+                words = e_rows[r, h][:].bitcast(F32)
+                for u in range(2):
+                    nc.tensor.transpose(e_t_bank[r, pair][:, j, u, :], words[:, P * u : P * u + P], ident_f32[:])
+
+        def keep_e_t(r, pair):
+            if not live(r):
+                return
+            if pair == PAIRS[0]:
+                e_grouped[r] = work.tile([P, GROUP, P, PACK], BF16, name="e_grouped", align_bytes=64)
+            nc.scalar.copy(
+                out=e_grouped[r][:].bitcast(F32)[:, pair[0] : pair[1] + 1],
+                in_=e_t_bank[r, pair][:].rearrange("p j u q -> p j q u"),
+            )
+
+        def quantise_e(r):
+            if not live(r):
+                return
+            e_codes[r] = work.tile([P, GROUP * P], U32, name="e_codes", align_bytes=64)
+            e_scales[r] = work.tile([P, GROUP * P], U8, name="e_scales", align_bytes=64)
+            nc.vector.quantize_mx(
+                out=e_codes[r][:].bitcast(FP8X4),
+                scales=e_scales[r][:],
+                in_=e_grouped[r][:].rearrange("p h q t -> p (h q t)"),
+            )
+
+        def weighted_sum(r):
+            if not live(r):
+                return
+            g = r // Q_BLOCKS
+            out_bank[r] = psum.tile([P, GROUP, D], F32, name="out_bank")
+            for h in range(GROUP):
+                queries = slice(P * h, P * h + P)
+                nc.tensor.matmul_mx(
+                    out=out_bank[r][:, h, :],
+                    lhsT=e_codes[r][:, queries].bitcast(FP8X4),
+                    lhsT_scale=e_scales[r][:, queries],
+                    rhs=v_codes[g][:, h, :].bitcast(FP8X4),
+                    rhs_scale=v_scales[g][:, h, :],
+                    start=True,
+                    stop=True,
+                )
+
+        def normalise_and_store(r):
+            if not live(r):
+                return
+            g, i = divmod(r, Q_BLOCKS)
+            inverse = work.tile([P, GROUP], F32, name="inverse")
+            nc.vector.reciprocal(out=inverse[:], in_=row_sum[r][:])
+            result = work.tile([P, GROUP, D], F32, name="result", bufs=3)
+            nc.vector.tensor_tensor(
+                out=result[:], in0=out_bank[r][:], in1=inverse[:].unsqueeze(2).to_broadcast([P, GROUP, D]), op=MULT
+            )
+            nc.sync.dma_start(out=out[0, P * i : P * i + P, GROUP * g : GROUP * g + GROUP, :], in_=result[:])
+
+        load_group(0)
+        load_group(1)
+        for b in range(Q_BLOCKS):
+            transpose_qk(0, b)
+            keep_q(0, b)
+            keep_k(0, b)
+            group_v(0, b)
+            quantise_v(0, b)
+        for h in range(GROUP):
+            score(0, h)
+
+        for r in range(ROUNDS + 2):
+            g, i = divmod(r, Q_BLOCKS)
+            first, second = PAIRS
+            if i == 0:
+                load_group(g + 2)
+            transpose_qk(g + 1, i)
+            row_max(r, first)
+            exponent(r, first)
+            score(r + 1, 0)
+            score(r + 1, 1)
+            transpose_e(r, first)
+            group_v(g + 1, i)
+            normalise_and_store(r - 2)
+            keep_e_t(r - 1, second)
+            keep_q(g + 1, i)
+            row_max(r, second)
+            exponent(r, second)
+            quantise_e(r - 1)
+            quantise_v(g + 1, i)
+            score(r + 1, 2)
+            weighted_sum(r - 1)
+            score(r + 1, 3)
+            transpose_e(r, second)
+            keep_e_t(r, first)
+            keep_k(g + 1, i)

@@ -11,6 +11,7 @@ FP8X4 = mybir.dt.float8_e4m3fn_x4
 EXP = mybir.ActivationFunctionType.Exp
 MAX = mybir.AluOpType.max
 MULT = mybir.AluOpType.mult
+ADD = mybir.AluOpType.add
 X = mybir.AxisListType.X
 
 P = 128
@@ -25,6 +26,7 @@ GROUP = 4
 GROUPS = HEADS // GROUP
 ROUNDS = GROUPS * Q_BLOCKS
 PAIRS = ((0, 1), (2, 3))
+SCORE_BANKS = 4
 SCALE = 1.0 / math.sqrt(D)
 
 FLOPS = 2 * 2 * HEADS * POSITIONS * KEYS * D
@@ -37,7 +39,9 @@ def tile_attention_kernel(tc, qkv, kv_seq_len, out):
 
     with tc.tile_pool(name="const", bufs=1) as const, tc.tile_pool(name="raw", bufs=3) as raw, tc.tile_pool(
         name="group", bufs=2
-    ) as group, tc.tile_pool(name="work", bufs=2) as work, tc.psum_pool(name="psum", bufs=1) as psum:
+    ) as group, tc.tile_pool(name="work", bufs=2) as work, tc.psum_pool(
+        name="psum", bufs=1
+    ) as psum, tc.manual_schedule():
         ident_bf16 = const.tile([P, P], BF16)
         make_identity(nc, ident_bf16[:])
         ident_f32 = const.tile([P, P], F32)
@@ -54,6 +58,7 @@ def tile_attention_kernel(tc, qkv, kv_seq_len, out):
         scores = {}
         e_rows = {}
         neg_max = {}
+        inverse = {}
         row_sum = {}
         e_t_bank = {}
         e_grouped = {}
@@ -67,26 +72,29 @@ def tile_attention_kernel(tc, qkv, kv_seq_len, out):
             heads = slice(GROUP * g, GROUP * g + GROUP)
             qk_raw[g] = raw.tile([P, Q_BLOCKS, GROUP, 2 * D], BF16, name="qk_raw")
             v_raw[g] = raw.tile([P, PACK, GROUP, D], BF16, name="v_raw")
-            for b in range(K_BLOCKS):
-                nc.sync.dma_start(out=qk_raw[g][:, b], in_=qkv[0, P * b : P * b + P, heads, 0 : 2 * D])
             for t in range(PACK):
                 first = 256 * (t // 2) + t % 2
                 nc.sync.dma_start(out=v_raw[g][:, t], in_=qkv[0, first : first + 256 : 2, heads, 2 * D : 3 * D])
+            for b in range(K_BLOCKS):
+                nc.sync.dma_start(out=qk_raw[g][:, b], in_=qkv[0, P * b : P * b + P, heads, 0 : 2 * D])
             b = K_BLOCKS
             nc.sync.dma_start(out=qk_raw[g][:, b, :, 0:D], in_=qkv[0, P * b : P * b + P, heads, 0:D])
 
         def open_group(g):
+            if g >= GROUPS:
+                return
             q_t[g] = group.tile([P, Q_BLOCKS, GROUP, P], BF16, name="q_t")
             k_t[g] = group.tile([P, GROUP, K_BLOCKS, P], BF16, name="k_t")
             v_codes[g] = group.tile([P, GROUP, D], U32, name="v_codes", align_bytes=64)
             v_scales[g] = group.tile([P, GROUP, D], U8, name="v_scales", align_bytes=64)
 
-        def transpose_qk(g, b):
+        def transpose_qk(g, b, before_rounds=False):
             if g >= GROUPS:
                 return
-            if b == 0:
-                open_group(g)
-            prep_bank[g, b] = psum.tile([P, 2, GROUP, P], BF16, name="prep_bank")
+            if before_rounds:
+                prep_bank[g, b] = psum.tile([P, 2, GROUP, P], BF16, name="prep_bank", tag="scores", bufs=SCORE_BANKS)
+            else:
+                prep_bank[g, b] = psum.tile([P, 2, GROUP, P], BF16, name="prep_bank")
             for part in range(2 if b < K_BLOCKS else 1):
                 for h in range(GROUP):
                     nc.tensor.transpose(
@@ -99,12 +107,19 @@ def tile_attention_kernel(tc, qkv, kv_seq_len, out):
 
         def keep_k(g, b):
             if g < GROUPS and b < K_BLOCKS:
-                nc.scalar.copy(out=k_t[g][:, :, b, :], in_=prep_bank[g, b][:, 1])
+                nc.vector.tensor_copy(out=k_t[g][:, :, b, :], in_=prep_bank[g, b][:, 1])
 
-        def group_v(g, h):
+        def group_v(g, h, engine):
             if g < GROUPS and h < GROUP:
-                v_grouped[g, h] = work.tile([P, D, PACK], BF16, name="v_grouped", align_bytes=64)
-                nc.vector.tensor_copy(out=v_grouped[g, h][:], in_=v_raw[g][:, :, h, :].rearrange("p t d -> p d t"))
+                v_grouped[g, h] = work.tile([P, D, PACK], BF16, name="v_grouped", align_bytes=64, bufs=4)
+                engine.tensor_scalar(
+                    out=v_grouped[g, h][:],
+                    in0=v_raw[g][:, :, h, :].rearrange("p t d -> p d t"),
+                    scalar1=1.0,
+                    scalar2=0.0,
+                    op0=MULT,
+                    op1=ADD,
+                )
 
         def quantise_v(g, h):
             if g < GROUPS and h < GROUP:
@@ -121,7 +136,7 @@ def tile_attention_kernel(tc, qkv, kv_seq_len, out):
             if not live(r):
                 return
             g, i = divmod(r, Q_BLOCKS)
-            scores[r, h] = psum.tile([P, KEYS], F32, name="scores", bufs=4)
+            scores[r, h] = psum.tile([P, KEYS], F32, name="scores", bufs=SCORE_BANKS)
             nc.tensor.matmul(
                 out=scores[r, h][:],
                 lhsT=q_t[g][:, i, h, :],
@@ -133,24 +148,24 @@ def tile_attention_kernel(tc, qkv, kv_seq_len, out):
         def row_max(r, pair):
             if not live(r):
                 return
-            top = work.tile([P, 2], F32, name="top", bufs=4)
-            for j, h in enumerate(pair):
-                nc.vector.tensor_reduce(out=top[:, j : j + 1], in_=scores[r, h][:], axis=X, op=MAX)
-            neg_max[r, pair] = work.tile([P, 2], F32, name="neg_max", bufs=4)
-            nc.vector.tensor_scalar_mul(out=neg_max[r, pair][:], in0=top[:], scalar1=-SCALE)
+            for h in pair:
+                top = work.tile([P, 1], F32, name="top", bufs=8)
+                nc.vector.tensor_reduce(out=top[:], in_=scores[r, h][:], axis=X, op=MAX)
+                neg_max[r, h] = work.tile([P, 1], F32, name="neg_max", bufs=8)
+                nc.gpsimd.tensor_scalar_mul(out=neg_max[r, h][:], in0=top[:], scalar1=-SCALE)
 
         def exponent(r, pair):
             if not live(r):
                 return
             if pair == PAIRS[0]:
                 row_sum[r] = work.tile([P, GROUP], F32, name="row_sum", bufs=4)
-            for j, h in enumerate(pair):
+            for h in pair:
                 e_rows[r, h] = work.tile([P, KEYS], BF16, name="e_rows", bufs=6)
                 nc.scalar.activation(
                     out=e_rows[r, h][:],
                     in_=scores[r, h][:],
                     func=EXP,
-                    bias=neg_max[r, pair][:, j : j + 1],
+                    bias=neg_max[r, h][:],
                     scale=SCALE,
                     accum_out=row_sum[r][:, h : h + 1],
                 )
@@ -202,51 +217,61 @@ def tile_attention_kernel(tc, qkv, kv_seq_len, out):
                     stop=True,
                 )
 
+        def invert_row_sum(r):
+            if live(r):
+                inverse[r] = work.tile([P, GROUP], F32, name="inverse", bufs=3)
+                nc.vector.reciprocal(out=inverse[r][:], in_=row_sum[r][:])
+
         def normalise_and_store(r):
             if not live(r):
                 return
             g, i = divmod(r, Q_BLOCKS)
-            inverse = work.tile([P, GROUP], F32, name="inverse")
-            nc.vector.reciprocal(out=inverse[:], in_=row_sum[r][:])
             result = work.tile([P, GROUP, D], F32, name="result", bufs=3)
             nc.vector.tensor_tensor(
-                out=result[:], in0=out_bank[r][:], in1=inverse[:].unsqueeze(2).to_broadcast([P, GROUP, D]), op=MULT
+                out=result[:], in0=out_bank[r][:], in1=inverse[r][:].unsqueeze(2).to_broadcast([P, GROUP, D]), op=MULT
             )
             nc.sync.dma_start(out=out[0, P * i : P * i + P, GROUP * g : GROUP * g + GROUP, :], in_=result[:])
 
         load_group(0)
         load_group(1)
-        for b in range(Q_BLOCKS):
-            transpose_qk(0, b)
+        open_group(0)
+        for h in range(GROUP):
+            group_v(0, h, nc.vector)
+        for h in range(GROUP):
+            quantise_v(0, h)
+        for b in range(K_BLOCKS):
+            transpose_qk(0, b, before_rounds=True)
             keep_q(0, b)
             keep_k(0, b)
-            group_v(0, b)
-            quantise_v(0, b)
         for h in range(GROUP):
             score(0, h)
+        transpose_qk(0, K_BLOCKS)
+        keep_q(0, K_BLOCKS)
 
         for r in range(ROUNDS + 2):
             g, i = divmod(r, Q_BLOCKS)
             first, second = PAIRS
             if i == 0:
                 load_group(g + 2)
+                open_group(g + 1)
             transpose_qk(g + 1, i)
             row_max(r, first)
             exponent(r, first)
             score(r + 1, 0)
             score(r + 1, 1)
             transpose_e(r, first)
-            group_v(g + 1, i)
+            group_v(g + 1, i, nc.gpsimd)
             normalise_and_store(r - 2)
             keep_e_t(r - 1, second)
             keep_q(g + 1, i)
             row_max(r, second)
             exponent(r, second)
+            keep_k(g + 1, i)
             quantise_e(r - 1)
             quantise_v(g + 1, i)
+            invert_row_sum(r - 1)
             score(r + 1, 2)
             weighted_sum(r - 1)
             score(r + 1, 3)
             transpose_e(r, second)
             keep_e_t(r, first)
-            keep_k(g + 1, i)

@@ -9,10 +9,9 @@ U32 = mybir.dt.uint32
 U8 = mybir.dt.uint8
 FP8X4 = mybir.dt.float8_e4m3fn_x4
 EXP = mybir.ActivationFunctionType.Exp
-MAX = mybir.AluOpType.max
+MIN = mybir.AluOpType.min
 MULT = mybir.AluOpType.mult
 ADD = mybir.AluOpType.add
-X = mybir.AxisListType.X
 
 P = 128
 PACK = 4
@@ -26,7 +25,7 @@ GROUP = 4
 GROUPS = HEADS // GROUP
 ROUNDS = GROUPS * Q_BLOCKS
 PAIRS = ((0, 1), (2, 3))
-SCORE_BANKS = 4
+SCORE_BANKS = 3
 SCALE = 1.0 / math.sqrt(D)
 
 FLOPS = 2 * 2 * HEADS * POSITIONS * KEYS * D
@@ -39,7 +38,7 @@ def tile_attention_kernel(tc, qkv, kv_seq_len, out):
 
     with tc.tile_pool(name="const", bufs=1) as const, tc.tile_pool(name="raw", bufs=3) as raw, tc.tile_pool(
         name="group", bufs=2
-    ) as group, tc.tile_pool(name="work", bufs=2) as work, tc.psum_pool(
+    ) as group, tc.tile_pool(name="work", bufs=3) as work, tc.psum_pool(
         name="psum", bufs=1
     ) as psum, tc.manual_schedule():
         ident_bf16 = const.tile([P, P], BF16)
@@ -51,15 +50,16 @@ def tile_attention_kernel(tc, qkv, kv_seq_len, out):
         v_raw = {}
         q_t = {}
         k_t = {}
+        v_grouped = {}
         v_codes = {}
         v_scales = {}
         prep_bank = {}
-        v_grouped = {}
         scores = {}
-        e_rows = {}
+        scaled = {}
         neg_max = {}
-        inverse = {}
+        e_rows = {}
         row_sum = {}
+        inverse = {}
         e_t_bank = {}
         e_grouped = {}
         e_codes = {}
@@ -72,11 +72,11 @@ def tile_attention_kernel(tc, qkv, kv_seq_len, out):
             heads = slice(GROUP * g, GROUP * g + GROUP)
             qk_raw[g] = raw.tile([P, Q_BLOCKS, GROUP, 2 * D], BF16, name="qk_raw")
             v_raw[g] = raw.tile([P, PACK, GROUP, D], BF16, name="v_raw")
+            for b in range(K_BLOCKS):
+                nc.sync.dma_start(out=qk_raw[g][:, b], in_=qkv[0, P * b : P * b + P, heads, 0 : 2 * D])
             for t in range(PACK):
                 first = 256 * (t // 2) + t % 2
                 nc.sync.dma_start(out=v_raw[g][:, t], in_=qkv[0, first : first + 256 : 2, heads, 2 * D : 3 * D])
-            for b in range(K_BLOCKS):
-                nc.sync.dma_start(out=qk_raw[g][:, b], in_=qkv[0, P * b : P * b + P, heads, 0 : 2 * D])
             b = K_BLOCKS
             nc.sync.dma_start(out=qk_raw[g][:, b, :, 0:D], in_=qkv[0, P * b : P * b + P, heads, 0:D])
 
@@ -85,6 +85,7 @@ def tile_attention_kernel(tc, qkv, kv_seq_len, out):
                 return
             q_t[g] = group.tile([P, Q_BLOCKS, GROUP, P], BF16, name="q_t")
             k_t[g] = group.tile([P, GROUP, K_BLOCKS, P], BF16, name="k_t")
+            v_grouped[g] = group.tile([P, GROUP, D, PACK], BF16, name="v_grouped", align_bytes=64)
             v_codes[g] = group.tile([P, GROUP, D], U32, name="v_codes", align_bytes=64)
             v_scales[g] = group.tile([P, GROUP, D], U8, name="v_scales", align_bytes=64)
 
@@ -105,15 +106,14 @@ def tile_attention_kernel(tc, qkv, kv_seq_len, out):
             if g < GROUPS:
                 nc.scalar.copy(out=q_t[g][:, b], in_=prep_bank[g, b][:, 0])
 
-        def keep_k(g, b):
+        def keep_k(g, b, engine):
             if g < GROUPS and b < K_BLOCKS:
-                nc.vector.tensor_copy(out=k_t[g][:, :, b, :], in_=prep_bank[g, b][:, 1])
+                engine(out=k_t[g][:, :, b, :], in_=prep_bank[g, b][:, 1])
 
-        def group_v(g, h, engine):
+        def group_v(g, h):
             if g < GROUPS and h < GROUP:
-                v_grouped[g, h] = work.tile([P, D, PACK], BF16, name="v_grouped", align_bytes=64, bufs=4)
-                engine.tensor_scalar(
-                    out=v_grouped[g, h][:],
+                nc.gpsimd.tensor_scalar(
+                    out=v_grouped[g][:, h],
                     in0=v_raw[g][:, :, h, :].rearrange("p t d -> p d t"),
                     scalar1=1.0,
                     scalar2=0.0,
@@ -121,13 +121,12 @@ def tile_attention_kernel(tc, qkv, kv_seq_len, out):
                     op1=ADD,
                 )
 
-        def quantise_v(g, h):
-            if g < GROUPS and h < GROUP:
-                nc.vector.quantize_mx(
-                    out=v_codes[g][:, h, :].bitcast(FP8X4),
-                    scales=v_scales[g][:, h, :],
-                    in_=v_grouped[g, h][:].rearrange("p d t -> p (d t)"),
-                )
+        def quantise_v(g):
+            nc.vector.quantize_mx(
+                out=v_codes[g][:].rearrange("p h d -> p (h d)").bitcast(FP8X4),
+                scales=v_scales[g][:].rearrange("p h d -> p (h d)"),
+                in_=v_grouped[g][:].rearrange("p h d t -> p (h d t)"),
+            )
 
         def live(r):
             return 0 <= r < ROUNDS
@@ -145,35 +144,40 @@ def tile_attention_kernel(tc, qkv, kv_seq_len, out):
                 stop=True,
             )
 
-        def row_max(r, pair):
+        def scale_and_max(r, h):
             if not live(r):
                 return
-            for h in pair:
-                top = work.tile([P, 1], F32, name="top", bufs=8)
-                nc.vector.tensor_reduce(out=top[:], in_=scores[r, h][:], axis=X, op=MAX)
-                neg_max[r, h] = work.tile([P, 1], F32, name="neg_max", bufs=8)
-                nc.gpsimd.tensor_scalar_mul(out=neg_max[r, h][:], in0=top[:], scalar1=-SCALE)
+            scaled[r, h] = work.tile([P, KEYS], F32, name="scaled", bufs=8)
+            neg_max[r, h] = work.tile([P, 1], F32, name="neg_max", bufs=8)
+            nc.vector.tensor_scalar(
+                out=scaled[r, h][:],
+                in0=scores[r, h][:],
+                scalar1=-SCALE,
+                scalar2=None,
+                op0=MULT,
+                op1=MIN,
+                accum_out=neg_max[r, h][:],
+            )
 
-        def exponent(r, pair):
+        def exponent(r, h):
             if not live(r):
                 return
-            if pair == PAIRS[0]:
+            if h == 0:
                 row_sum[r] = work.tile([P, GROUP], F32, name="row_sum", bufs=4)
-            for h in pair:
-                e_rows[r, h] = work.tile([P, KEYS], BF16, name="e_rows", bufs=6)
-                nc.scalar.activation(
-                    out=e_rows[r, h][:],
-                    in_=scores[r, h][:],
-                    func=EXP,
-                    bias=neg_max[r, h][:],
-                    scale=SCALE,
-                    accum_out=row_sum[r][:, h : h + 1],
-                )
+            e_rows[r, h] = work.tile([P, KEYS], BF16, name="e_rows", bufs=8)
+            nc.scalar.activation(
+                out=e_rows[r, h][:],
+                in_=scaled[r, h][:],
+                func=EXP,
+                bias=neg_max[r, h][:],
+                scale=-1.0,
+                accum_out=row_sum[r][:, h : h + 1],
+            )
 
         def transpose_e(r, pair):
             if not live(r):
                 return
-            e_t_bank[r, pair] = psum.tile([P, 2, 2, P], F32, name="e_t_bank", bufs=2)
+            e_t_bank[r, pair] = psum.tile([P, 2, 2, P], F32, name="e_t_bank", bufs=3)
             for j, h in enumerate(pair):
                 words = e_rows[r, h][:].bitcast(F32)
                 for u in range(2):
@@ -192,6 +196,8 @@ def tile_attention_kernel(tc, qkv, kv_seq_len, out):
         def quantise_e(r):
             if not live(r):
                 return
+            if r % Q_BLOCKS == 0:
+                quantise_v(r // Q_BLOCKS)
             e_codes[r] = work.tile([P, GROUP * P], U32, name="e_codes", align_bytes=64)
             e_scales[r] = work.tile([P, GROUP * P], U8, name="e_scales", align_bytes=64)
             nc.vector.quantize_mx(
@@ -199,6 +205,8 @@ def tile_attention_kernel(tc, qkv, kv_seq_len, out):
                 scales=e_scales[r][:],
                 in_=e_grouped[r][:].rearrange("p h q t -> p (h q t)"),
             )
+            inverse[r] = work.tile([P, GROUP], F32, name="inverse")
+            nc.vector.reciprocal(out=inverse[r][:], in_=row_sum[r][:])
 
         def weighted_sum(r):
             if not live(r):
@@ -217,16 +225,11 @@ def tile_attention_kernel(tc, qkv, kv_seq_len, out):
                     stop=True,
                 )
 
-        def invert_row_sum(r):
-            if live(r):
-                inverse[r] = work.tile([P, GROUP], F32, name="inverse", bufs=3)
-                nc.vector.reciprocal(out=inverse[r][:], in_=row_sum[r][:])
-
         def normalise_and_store(r):
             if not live(r):
                 return
             g, i = divmod(r, Q_BLOCKS)
-            result = work.tile([P, GROUP, D], F32, name="result", bufs=3)
+            result = work.tile([P, GROUP, D], F32, name="result")
             nc.vector.tensor_tensor(
                 out=result[:], in0=out_bank[r][:], in1=inverse[r][:].unsqueeze(2).to_broadcast([P, GROUP, D]), op=MULT
             )
@@ -235,43 +238,42 @@ def tile_attention_kernel(tc, qkv, kv_seq_len, out):
         load_group(0)
         load_group(1)
         open_group(0)
-        for h in range(GROUP):
-            group_v(0, h, nc.vector)
-        for h in range(GROUP):
-            quantise_v(0, h)
         for b in range(K_BLOCKS):
             transpose_qk(0, b, before_rounds=True)
             keep_q(0, b)
-            keep_k(0, b)
+            keep_k(0, b, nc.vector.tensor_copy)
         for h in range(GROUP):
             score(0, h)
+            group_v(0, h)
         transpose_qk(0, K_BLOCKS)
         keep_q(0, K_BLOCKS)
 
-        for r in range(ROUNDS + 2):
+        for r in range(ROUNDS + 3):
             g, i = divmod(r, Q_BLOCKS)
             first, second = PAIRS
             if i == 0:
                 load_group(g + 2)
                 open_group(g + 1)
+            transpose_e(r - 1, first)
+            transpose_e(r - 1, second)
             transpose_qk(g + 1, i)
-            row_max(r, first)
-            exponent(r, first)
+            group_v(g + 1, i)
+            scale_and_max(r, 0)
+            scale_and_max(r, 1)
+            exponent(r, 0)
+            exponent(r, 1)
             score(r + 1, 0)
             score(r + 1, 1)
-            transpose_e(r, first)
-            group_v(g + 1, i, nc.gpsimd)
-            normalise_and_store(r - 2)
-            keep_e_t(r - 1, second)
+            quantise_e(r - 2)
+            weighted_sum(r - 2)
+            keep_e_t(r - 1, first)
             keep_q(g + 1, i)
-            row_max(r, second)
-            exponent(r, second)
-            keep_k(g + 1, i)
-            quantise_e(r - 1)
-            quantise_v(g + 1, i)
-            invert_row_sum(r - 1)
+            scale_and_max(r, 2)
+            scale_and_max(r, 3)
+            exponent(r, 2)
+            exponent(r, 3)
             score(r + 1, 2)
-            weighted_sum(r - 1)
             score(r + 1, 3)
-            transpose_e(r, second)
-            keep_e_t(r, first)
+            normalise_and_store(r - 3)
+            keep_e_t(r - 1, second)
+            keep_k(g + 1, i, nc.scalar.copy)

@@ -26,6 +26,8 @@ GROUPS = HEADS // GROUP
 ROUNDS = GROUPS * Q_BLOCKS
 PAIRS = ((0, 1), (2, 3))
 SCORE_BANKS = 3
+Q_LEAD = 2
+NO_ROUND = -1
 SCALE = 1.0 / math.sqrt(D)
 
 FLOPS = 2 * 2 * HEADS * POSITIONS * KEYS * D
@@ -53,7 +55,8 @@ def tile_attention_kernel(tc, qkv, kv_seq_len, out):
         v_grouped = {}
         v_codes = {}
         v_scales = {}
-        prep_bank = {}
+        q_bank = {}
+        k_bank = {}
         scores = {}
         scaled = {}
         neg_max = {}
@@ -65,6 +68,9 @@ def tile_attention_kernel(tc, qkv, kv_seq_len, out):
         e_codes = {}
         e_scales = {}
         out_bank = {}
+
+        def live(r):
+            return 0 <= r < ROUNDS
 
         def load_group(g):
             if g >= GROUPS:
@@ -83,32 +89,40 @@ def tile_attention_kernel(tc, qkv, kv_seq_len, out):
         def open_group(g):
             if g >= GROUPS:
                 return
-            q_t[g] = group.tile([P, Q_BLOCKS, GROUP, P], BF16, name="q_t")
             k_t[g] = group.tile([P, GROUP, K_BLOCKS, P], BF16, name="k_t")
             v_grouped[g] = group.tile([P, GROUP, D, PACK], BF16, name="v_grouped", align_bytes=64)
             v_codes[g] = group.tile([P, GROUP, D], U32, name="v_codes", align_bytes=64)
             v_scales[g] = group.tile([P, GROUP, D], U8, name="v_scales", align_bytes=64)
 
-        def transpose_qk(g, b, before_rounds=False):
-            if g >= GROUPS:
+        def transpose_qk(r, g, b, before_rounds=False):
+            with_q = live(r)
+            with_k = g < GROUPS and b < K_BLOCKS
+            if not (with_q or with_k):
                 return
             if before_rounds:
-                prep_bank[g, b] = psum.tile([P, 2, GROUP, P], BF16, name="prep_bank", tag="scores", bufs=SCORE_BANKS)
+                bank = psum.tile([P, 2, GROUP, P], BF16, name="prep_bank", tag="scores", bufs=SCORE_BANKS)
             else:
-                prep_bank[g, b] = psum.tile([P, 2, GROUP, P], BF16, name="prep_bank")
-            for part in range(2 if b < K_BLOCKS else 1):
+                bank = psum.tile([P, 2, GROUP, P], BF16, name="prep_bank")
+            if with_q:
+                q_bank[r] = bank
                 for h in range(GROUP):
-                    nc.tensor.transpose(
-                        prep_bank[g, b][:, part, h, :], qk_raw[g][:, b, h, D * part : D * part + D], ident_bf16[:]
-                    )
+                    nc.tensor.transpose(bank[:, 0, h, :], qk_raw[r // Q_BLOCKS][:, r % Q_BLOCKS, h, 0:D], ident_bf16[:])
+            if with_k:
+                k_bank[g, b] = bank
+                for h in range(GROUP):
+                    nc.tensor.transpose(bank[:, 1, h, :], qk_raw[g][:, b, h, D : 2 * D], ident_bf16[:])
 
-        def keep_q(g, b):
-            if g < GROUPS:
-                nc.scalar.copy(out=q_t[g][:, b], in_=prep_bank[g, b][:, 0])
+        def keep_q(r):
+            if live(r):
+                q_t[r] = work.tile([P, GROUP, P], BF16, name="q_t", bufs=4)
+                nc.scalar.copy(out=q_t[r][:], in_=q_bank[r][:, 0])
 
-        def keep_k(g, b, engine):
+        def keep_k(g, b):
             if g < GROUPS and b < K_BLOCKS:
-                engine(out=k_t[g][:, :, b, :], in_=prep_bank[g, b][:, 1])
+                if b % 2 == 0:
+                    nc.vector.tensor_copy(out=k_t[g][:, :, b, :], in_=k_bank[g, b][:, 1])
+                else:
+                    nc.scalar.copy(out=k_t[g][:, :, b, :], in_=k_bank[g, b][:, 1])
 
         def group_v(g, h):
             if g < GROUPS and h < GROUP:
@@ -128,17 +142,14 @@ def tile_attention_kernel(tc, qkv, kv_seq_len, out):
                 in_=v_grouped[g][:].rearrange("p h d t -> p (h d t)"),
             )
 
-        def live(r):
-            return 0 <= r < ROUNDS
-
         def score(r, h):
             if not live(r):
                 return
-            g, i = divmod(r, Q_BLOCKS)
+            g = r // Q_BLOCKS
             scores[r, h] = psum.tile([P, KEYS], F32, name="scores", bufs=SCORE_BANKS)
             nc.tensor.matmul(
                 out=scores[r, h][:],
-                lhsT=q_t[g][:, i, h, :],
+                lhsT=q_t[r][:, h, :],
                 rhs=k_t[g][:, h].rearrange("d b k -> d (b k)"),
                 start=True,
                 stop=True,
@@ -163,7 +174,7 @@ def tile_attention_kernel(tc, qkv, kv_seq_len, out):
             if not live(r):
                 return
             if h == 0:
-                row_sum[r] = work.tile([P, GROUP], F32, name="row_sum", bufs=4)
+                row_sum[r] = work.tile([P, GROUP], F32, name="row_sum", bufs=5)
             e_rows[r, h] = work.tile([P, KEYS], BF16, name="e_rows", bufs=8)
             nc.scalar.activation(
                 out=e_rows[r, h][:],
@@ -187,7 +198,7 @@ def tile_attention_kernel(tc, qkv, kv_seq_len, out):
             if not live(r):
                 return
             if pair == PAIRS[0]:
-                e_grouped[r] = work.tile([P, GROUP, P, PACK], BF16, name="e_grouped", align_bytes=64)
+                e_grouped[r] = work.tile([P, GROUP, P, PACK], BF16, name="e_grouped", align_bytes=64, bufs=4)
             nc.scalar.copy(
                 out=e_grouped[r][:].bitcast(F32)[:, pair[0] : pair[1] + 1],
                 in_=e_t_bank[r, pair][:].rearrange("p j u q -> p j q u"),
@@ -239,16 +250,15 @@ def tile_attention_kernel(tc, qkv, kv_seq_len, out):
         load_group(1)
         open_group(0)
         for b in range(K_BLOCKS):
-            transpose_qk(0, b, before_rounds=True)
-            keep_q(0, b)
-            keep_k(0, b, nc.vector.tensor_copy)
+            early = b if b < Q_LEAD else NO_ROUND
+            transpose_qk(early, 0, b, before_rounds=True)
+            keep_k(0, b)
+            keep_q(early)
         for h in range(GROUP):
             score(0, h)
             group_v(0, h)
-        transpose_qk(0, K_BLOCKS)
-        keep_q(0, K_BLOCKS)
 
-        for r in range(ROUNDS + 3):
+        for r in range(ROUNDS + 4):
             g, i = divmod(r, Q_BLOCKS)
             first, second = PAIRS
             if i == 0:
@@ -256,7 +266,7 @@ def tile_attention_kernel(tc, qkv, kv_seq_len, out):
                 open_group(g + 1)
             transpose_e(r - 1, first)
             transpose_e(r - 1, second)
-            transpose_qk(g + 1, i)
+            transpose_qk(r + Q_LEAD, g + 1, i)
             group_v(g + 1, i)
             scale_and_max(r, 0)
             scale_and_max(r, 1)
@@ -264,16 +274,16 @@ def tile_attention_kernel(tc, qkv, kv_seq_len, out):
             exponent(r, 1)
             score(r + 1, 0)
             score(r + 1, 1)
-            quantise_e(r - 2)
-            weighted_sum(r - 2)
+            quantise_e(r - 3)
+            weighted_sum(r - 3)
             keep_e_t(r - 1, first)
-            keep_q(g + 1, i)
+            keep_q(r + Q_LEAD)
             scale_and_max(r, 2)
             scale_and_max(r, 3)
             exponent(r, 2)
             exponent(r, 3)
             score(r + 1, 2)
             score(r + 1, 3)
-            normalise_and_store(r - 3)
+            normalise_and_store(r - 4)
             keep_e_t(r - 1, second)
-            keep_k(g + 1, i, nc.scalar.copy)
+            keep_k(g + 1, i)

@@ -40,9 +40,7 @@ def tile_attention_kernel(tc, qkv, kv_seq_len, out):
 
     with tc.tile_pool(name="const", bufs=1) as const, tc.tile_pool(name="raw", bufs=3) as raw, tc.tile_pool(
         name="group", bufs=2
-    ) as group, tc.tile_pool(name="work", bufs=3) as work, tc.psum_pool(
-        name="psum", bufs=1
-    ) as psum, tc.manual_schedule():
+    ) as group, tc.tile_pool(name="work", bufs=3) as work, tc.psum_pool(name="psum", bufs=1) as psum:
         ident_bf16 = const.tile([P, P], BF16)
         make_identity(nc, ident_bf16[:])
         ident_f32 = const.tile([P, P], F32)

import math

import concourse.mybir as mybir
from concourse.masks import make_identity

F32 = mybir.dt.float32
BF16 = mybir.dt.bfloat16
U32 = mybir.dt.uint32
U8 = mybir.dt.uint8
FP8X4 = mybir.dt.float8_e4m3fn_x4
EXP = mybir.ActivationFunctionType.Exp
MIN = mybir.AluOpType.min
MULT = mybir.AluOpType.mult
ADD = mybir.AluOpType.add

P = 128
PACK = 4
POSITIONS = 640
HEADS = 32
D = 128
KEYS = 512
Q_BLOCKS = POSITIONS // P
K_BLOCKS = KEYS // P
GROUP = 4
GROUPS = HEADS // GROUP
ROUNDS = GROUPS * Q_BLOCKS
PAIRS = ((0, 1), (2, 3))
SCORE_BANKS = 3
Q_LEAD = 2
NO_ROUND = -1
SCALE = 1.0 / math.sqrt(D)

FLOPS = 2 * 2 * HEADS * POSITIONS * KEYS * D
BYTES = 2 * HEADS * D * (POSITIONS + 2 * KEYS) + 4 * HEADS * D * POSITIONS


def tile_attention_kernel(tc, qkv, kv_seq_len, out):
    nc = tc.nc
    assert kv_seq_len == KEYS

    with tc.tile_pool(name="const", bufs=1) as const, tc.tile_pool(name="raw", bufs=3) as raw, tc.tile_pool(
        name="group", bufs=2
    ) as group, tc.tile_pool(name="work", bufs=3) as work, tc.psum_pool(name="psum", bufs=1) as psum:
        ident_bf16 = const.tile([P, P], BF16)
        make_identity(nc, ident_bf16[:])
        ident_f32 = const.tile([P, P], F32)
        make_identity(nc, ident_f32[:])

        qk_raw = {}
        v_raw = {}
        q_t = {}
        k_t = {}
        v_grouped = {}
        v_codes = {}
        v_scales = {}
        q_bank = {}
        k_bank = {}
        scores = {}
        scaled = {}
        neg_max = {}
        e_rows = {}
        row_sum = {}
        inverse = {}
        e_t_bank = {}
        e_grouped = {}
        e_codes = {}
        e_scales = {}
        out_bank = {}

        def live(r):
            return 0 <= r < ROUNDS

        def load_group(g):
            if g >= GROUPS:
                return
            heads = slice(GROUP * g, GROUP * g + GROUP)
            qk_raw[g] = raw.tile([P, Q_BLOCKS, GROUP, 2 * D], BF16, name="qk_raw")
            v_raw[g] = raw.tile([P, PACK, GROUP, D], BF16, name="v_raw")
            for b in range(K_BLOCKS):
                nc.sync.dma_start(out=qk_raw[g][:, b], in_=qkv[0, P * b : P * b + P, heads, 0 : 2 * D])
            for t in range(PACK):
                first = 256 * (t // 2) + t % 2
                nc.sync.dma_start(out=v_raw[g][:, t], in_=qkv[0, first : first + 256 : 2, heads, 2 * D : 3 * D])
            b = K_BLOCKS
            nc.sync.dma_start(out=qk_raw[g][:, b, :, 0:D], in_=qkv[0, P * b : P * b + P, heads, 0:D])

        def open_group(g):
            if g >= GROUPS:
                return
            k_t[g] = group.tile([P, GROUP, K_BLOCKS, P], BF16, name="k_t")
            v_grouped[g] = group.tile([P, GROUP, D, PACK], BF16, name="v_grouped", align_bytes=64)
            v_codes[g] = group.tile([P, GROUP, D], U32, name="v_codes", align_bytes=64)
            v_scales[g] = group.tile([P, GROUP, D], U8, name="v_scales", align_bytes=64)

        def transpose_qk(r, g, b, before_rounds=False):
            with_q = live(r)
            with_k = g < GROUPS and b < K_BLOCKS
            if not (with_q or with_k):
                return
            if before_rounds:
                bank = psum.tile([P, 2, GROUP, P], BF16, name="prep_bank", tag="scores", bufs=SCORE_BANKS)
            else:
                bank = psum.tile([P, 2, GROUP, P], BF16, name="prep_bank")
            if with_q:
                q_bank[r] = bank
                for h in range(GROUP):
                    nc.tensor.transpose(bank[:, 0, h, :], qk_raw[r // Q_BLOCKS][:, r % Q_BLOCKS, h, 0:D], ident_bf16[:])
            if with_k:
                k_bank[g, b] = bank
                for h in range(GROUP):
                    nc.tensor.transpose(bank[:, 1, h, :], qk_raw[g][:, b, h, D : 2 * D], ident_bf16[:])

        def keep_q(r):
            if live(r):
                q_t[r] = work.tile([P, GROUP, P], BF16, name="q_t", bufs=4)
                nc.scalar.copy(out=q_t[r][:], in_=q_bank[r][:, 0])

        def keep_k(g, b):
            if g < GROUPS and b < K_BLOCKS:
                if b % 2 == 0:
                    nc.vector.tensor_copy(out=k_t[g][:, :, b, :], in_=k_bank[g, b][:, 1])
                else:
                    nc.scalar.copy(out=k_t[g][:, :, b, :], in_=k_bank[g, b][:, 1])

        def group_v(g, h):
            if g < GROUPS and h < GROUP:
                nc.gpsimd.tensor_scalar(
                    out=v_grouped[g][:, h],
                    in0=v_raw[g][:, :, h, :].rearrange("p t d -> p d t"),
                    scalar1=1.0,
                    scalar2=0.0,
                    op0=MULT,
                    op1=ADD,
                )

        def quantise_v(g):
            nc.vector.quantize_mx(
                out=v_codes[g][:].rearrange("p h d -> p (h d)").bitcast(FP8X4),
                scales=v_scales[g][:].rearrange("p h d -> p (h d)"),
                in_=v_grouped[g][:].rearrange("p h d t -> p (h d t)"),
            )

        def score(r, h):
            if not live(r):
                return
            g = r // Q_BLOCKS
            scores[r, h] = psum.tile([P, KEYS], F32, name="scores", bufs=SCORE_BANKS)
            nc.tensor.matmul(
                out=scores[r, h][:],
                lhsT=q_t[r][:, h, :],
                rhs=k_t[g][:, h].rearrange("d b k -> d (b k)"),
                start=True,
                stop=True,
            )

        def scale_and_max(r, h):
            if not live(r):
                return
            scaled[r, h] = work.tile([P, KEYS], F32, name="scaled", bufs=8)
            neg_max[r, h] = work.tile([P, 1], F32, name="neg_max", bufs=8)
            nc.vector.tensor_scalar(
                out=scaled[r, h][:],
                in0=scores[r, h][:],
                scalar1=-SCALE,
                scalar2=None,
                op0=MULT,
                op1=MIN,
                accum_out=neg_max[r, h][:],
            )

        def exponent(r, h):
            if not live(r):
                return
            if h == 0:
                row_sum[r] = work.tile([P, GROUP], F32, name="row_sum", bufs=5)
            e_rows[r, h] = work.tile([P, KEYS], BF16, name="e_rows", bufs=8)
            nc.scalar.activation(
                out=e_rows[r, h][:],
                in_=scaled[r, h][:],
                func=EXP,
                bias=neg_max[r, h][:],
                scale=-1.0,
                accum_out=row_sum[r][:, h : h + 1],
            )

        def transpose_e(r, pair):
            if not live(r):
                return
            e_t_bank[r, pair] = psum.tile([P, 2, 2, P], F32, name="e_t_bank", bufs=3)
            for j, h in enumerate(pair):
                words = e_rows[r, h][:].bitcast(F32)
                for u in range(2):
                    nc.tensor.transpose(e_t_bank[r, pair][:, j, u, :], words[:, P * u : P * u + P], ident_f32[:])

        def keep_e_t(r, pair):
            if not live(r):
                return
            if pair == PAIRS[0]:
                e_grouped[r] = work.tile([P, GROUP, P, PACK], BF16, name="e_grouped", align_bytes=64, bufs=4)
            nc.scalar.copy(
                out=e_grouped[r][:].bitcast(F32)[:, pair[0] : pair[1] + 1],
                in_=e_t_bank[r, pair][:].rearrange("p j u q -> p j q u"),
            )

        def quantise_e(r):
            if not live(r):
                return
            if r % Q_BLOCKS == 0:
                quantise_v(r // Q_BLOCKS)
            e_codes[r] = work.tile([P, GROUP * P], U32, name="e_codes", align_bytes=64)
            e_scales[r] = work.tile([P, GROUP * P], U8, name="e_scales", align_bytes=64)
            nc.vector.quantize_mx(
                out=e_codes[r][:].bitcast(FP8X4),
                scales=e_scales[r][:],
                in_=e_grouped[r][:].rearrange("p h q t -> p (h q t)"),
            )
            inverse[r] = work.tile([P, GROUP], F32, name="inverse")
            nc.vector.reciprocal(out=inverse[r][:], in_=row_sum[r][:])

        def weighted_sum(r):
            if not live(r):
                return
            g = r // Q_BLOCKS
            out_bank[r] = psum.tile([P, GROUP, D], F32, name="out_bank")
            for h in range(GROUP):
                queries = slice(P * h, P * h + P)
                nc.tensor.matmul_mx(
                    out=out_bank[r][:, h, :],
                    lhsT=e_codes[r][:, queries].bitcast(FP8X4),
                    lhsT_scale=e_scales[r][:, queries],
                    rhs=v_codes[g][:, h, :].bitcast(FP8X4),
                    rhs_scale=v_scales[g][:, h, :],
                    start=True,
                    stop=True,
                )

        def normalise_and_store(r):
            if not live(r):
                return
            g, i = divmod(r, Q_BLOCKS)
            result = work.tile([P, GROUP, D], F32, name="result")
            nc.vector.tensor_tensor(
                out=result[:], in0=out_bank[r][:], in1=inverse[r][:].unsqueeze(2).to_broadcast([P, GROUP, D]), op=MULT
            )
            nc.sync.dma_start(out=out[0, P * i : P * i + P, GROUP * g : GROUP * g + GROUP, :], in_=result[:])

        load_group(0)
        load_group(1)
        open_group(0)
        for b in range(K_BLOCKS):
            early = b if b < Q_LEAD else NO_ROUND
            transpose_qk(early, 0, b, before_rounds=True)
            keep_k(0, b)
            keep_q(early)
        for h in range(GROUP):
            score(0, h)
            group_v(0, h)

        for r in range(ROUNDS + 4):
            g, i = divmod(r, Q_BLOCKS)
            first, second = PAIRS
            if i == 0:
                load_group(g + 2)
                open_group(g + 1)
            transpose_e(r - 1, first)
            transpose_e(r - 1, second)
            transpose_qk(r + Q_LEAD, g + 1, i)
            group_v(g + 1, i)
            scale_and_max(r, 0)
            scale_and_max(r, 1)
            exponent(r, 0)
            exponent(r, 1)
            score(r + 1, 0)
            score(r + 1, 1)
            quantise_e(r - 3)
            weighted_sum(r - 3)
            keep_e_t(r - 1, first)
            keep_q(r + Q_LEAD)
            scale_and_max(r, 2)
            scale_and_max(r, 3)
            exponent(r, 2)
            exponent(r, 3)
            score(r + 1, 2)
            score(r + 1, 3)
            normalise_and_store(r - 4)
            keep_e_t(r - 1, second)
            keep_k(g + 1, i)
